import numpy as np
import ml_dtypes


def mxq(x, axis, fmt="e4m3"):
    dtype, down = {"e4m3": (ml_dtypes.float8_e4m3fn, 7), "e5m2": (ml_dtypes.float8_e5m2, 14)}[fmt]
    v = np.moveaxis(np.asarray(x, np.float32).astype(ml_dtypes.bfloat16).astype(np.float64), axis, -1)
    blocks = v.reshape(v.shape[:-1] + (-1, 32))
    amax = np.abs(blocks).max(-1, keepdims=True)
    byte = np.maximum(np.where(amax > 0, np.frexp(amax)[1] - 1 + 127, 0) - down, 1)
    scale = np.exp2(byte - 127.0)
    codes = (blocks / scale).astype(np.float32).astype(dtype).astype(np.float64)
    return np.moveaxis((codes * scale).reshape(v.shape), -1, axis)


WIDE = False


def mx_kscale(k):
    if not WIDE:
        return np.ones(k)
    levels = np.array([10, -10, 5, -5, 0])
    a = np.random.permutation(np.resize(levels, k // 512 * 4)).reshape(k // 512, 4)
    idx = np.arange(k)
    return np.exp2(a[idx // 512, idx % 128 // 32])


BF16 = ml_dtypes.bfloat16


def bf(x):
    return np.asarray(x, np.float32).astype(BF16)


def f64(x):
    return np.asarray(x).astype(np.float64)


E2M1 = np.array([0.0, 0.5, 1.0, 1.5, 2.0, 3.0, 4.0, 6.0, -0.0, -0.5, -1.0, -1.5, -2.0, -3.0, -4.0, -6.0])


def pack_weight(w, fmt):
    k, n = w.shape
    w = f64(bf(w)).reshape(k // 32, 32, n)
    amax = np.abs(w).max(1)
    if fmt == "e4m3":
        byte = np.frexp(amax)[1] - 1 + 127 - 7
    else:
        mant, ex = np.frexp(amax / 6.0)
        byte = np.where(mant > 0.5, ex, ex - 1) + 127
    byte = np.clip(np.where(amax > 0, byte, 1), 1, 254)
    scaled = (w * np.exp2(127.0 - byte)[:, None, :]).reshape(k, n).astype(np.float32)
    by_word = np.ascontiguousarray(scaled.reshape(k // 512, 128, 4, n).transpose(0, 1, 3, 2))
    if fmt == "e4m3":
        words = by_word.astype(ml_dtypes.float8_e4m3fn).view(np.uint8)
    else:
        c = by_word.astype(ml_dtypes.float4_e2m1fn).view(np.uint8) & 0xF
        words = c[..., 0::2] | (c[..., 1::2] << 4)
    return np.ascontiguousarray(words), np.ascontiguousarray(byte.astype(np.uint8).reshape(k // 512, 16, n))


def unpack_weight(words, scales, fmt):
    g, p, n, _ = words.shape
    if fmt == "e4m3":
        vals = np.ascontiguousarray(words).view(ml_dtypes.float8_e4m3fn).astype(np.float64)
    else:
        nib = np.empty((g, p, n, 4), np.uint8)
        nib[..., 0::2] = words & 0xF
        nib[..., 1::2] = words >> 4
        vals = E2M1[nib]
    vals = vals * np.repeat(np.exp2(scales.astype(np.float64) - 127.0), 8, axis=1)[..., None]
    return vals.transpose(0, 1, 3, 2).reshape(g * 512, n)

def pack4(w):
    words, scales = pack_weight(w, "e2m1")
    return words.reshape(words.shape[0], 128, -1), scales


def unpack4(words, scales):
    return unpack_weight(words.reshape(words.shape[0], 128, -1, 2), scales, "e2m1")


BATCH, IN_F, OUT_F, RANK, N_ADAPTERS = 1024, 16384, 256, 128, 8
SEG = BATCH // N_ADAPTERS
LORA_GAIN = 2.0


def setup_inputs():
    s = mx_kscale(IN_F)
    x = bf(np.random.standard_normal((BATCH, IN_F)) * s)
    h_lora = bf(np.random.standard_normal((N_ADAPTERS, SEG, RANK)))
    lora_B = bf(np.random.standard_normal((N_ADAPTERS, RANK, OUT_F)) * 0.5 / np.sqrt(RANK))
    words, scales = pack4(np.random.standard_normal((IN_F, OUT_F)) / np.sqrt(IN_F) / s[:, None])
    return {"x": x,
            "h_lora": h_lora,
            "lora_B": lora_B,
            "M_words": words,
            "M_scales": scales}


def reference(x, h_lora, lora_B, M_words, M_scales):
    y = (f64(h_lora) @ f64(lora_B)) * LORA_GAIN
    y = y.reshape(BATCH, OUT_F)
    return y + (mxq(f64(x), 1, "e4m3") @ unpack4(M_words, M_scales))

@@ -1,0 +1,233 @@
+from contextlib import ExitStack
+
+import concourse.mybir as mybir
+from concourse.masks import make_identity
+
+F32 = mybir.dt.float32
+BF16 = mybir.dt.bfloat16
+I32 = mybir.dt.int32
+U32 = mybir.dt.uint32
+U8 = mybir.dt.uint8
+FP8X4 = mybir.dt.float8_e4m3fn_x4
+FP4X4 = mybir.dt.float4_e2m1fn_x4
+ALU = mybir.AluOpType
+
+P = 128
+BATCH, IN_F, OUT_F, RANK, N_ADAPTERS = 1024, 16384, 256, 128, 8
+LORA_GAIN = 2.0
+
+K_PASS = 4 * P
+PASSES = IN_F // K_PASS
+ROWS = 512
+BLOCKS = ROWS // P
+HALVES = BATCH // ROWS
+OUT_TILES = OUT_F // P
+PAIR = 2
+UNIT_PAIRS = 2
+UNIT_PASSES = PAIR * UNIT_PAIRS
+K_UNIT = UNIT_PASSES * K_PASS
+UNITS_PER_HALF = IN_F // K_UNIT
+UNITS = HALVES * UNITS_PER_HALF
+RAW_UNITS = 3
+
+FLOPS = 2 * BATCH * IN_F * OUT_F + 2 * BATCH * RANK * OUT_F
+
+
+def tile_lorasequential_pa_k_kernel(tc, x, h_lora, lora_B, M_words, M_scales, out):
+    nc = tc.nc
+    with ExitStack() as ctx:
+        ctx.enter_context(tc.manual_schedule())
+        keep = ctx.enter_context(tc.tile_pool(name="keep", bufs=1))
+        raw_pool = ctx.enter_context(tc.tile_pool(name="raw", bufs=RAW_UNITS * BLOCKS))
+        sorted_pool = ctx.enter_context(tc.tile_pool(name="sorted", bufs=2 * BLOCKS))
+        mx_pool = ctx.enter_context(tc.tile_pool(name="mx", bufs=2 * UNIT_PAIRS))
+        end_pool = ctx.enter_context(tc.tile_pool(name="end", bufs=2))
+        banks = ctx.enter_context(tc.psum_pool(name="banks", bufs=6))
+        sums_pool = ctx.enter_context(tc.psum_pool(name="sums", bufs=1))
+
+        ident_f32 = keep.tile([P, P], F32)
+        make_identity(nc, ident_f32[:])
+        ident_bf16 = keep.tile([P, P], BF16)
+        make_identity(nc, ident_bf16[:])
+
+        m_words = keep.tile([P, PASSES, 2 * OUT_F], U8, align_bytes=64)
+        m_scales = keep.tile([P, PASSES, OUT_F], U8, align_bytes=64)
+        nc.vector.memset(m_scales[:].bitcast(I32), 0)
+
+        raw = {}
+        words = {}
+        grouped = {}
+        codes = {}
+        sums = {}
+        sums_sb = {}
+
+        def load_x(u):
+            half, c = divmod(u, UNITS_PER_HALF)
+            for b in range(BLOCKS):
+                r0 = half * ROWS + b * P
+                x_raw = raw_pool.tile([P, K_UNIT], BF16)
+                nc.sync.dma_start(out=x_raw[:], in_=x[r0 : r0 + P, c * K_UNIT : (c + 1) * K_UNIT])
+                raw[(u, b)] = x_raw
+
+        def load_m_words(c):
+            g0 = c * UNIT_PASSES
+            nc.sync.dma_start(
+                out=m_words[:, g0 : g0 + UNIT_PASSES, :].bitcast(I32),
+                in_=M_words.bitcast(I32)[g0 : g0 + UNIT_PASSES].rearrange("g p w -> p g w"),
+            )
+
+        def load_m_scales():
+            planes = m_scales[:].bitcast(I32)
+            rows = M_scales.bitcast(I32)
+            for g0 in range(0, PASSES, PASSES // 2):
+                g1 = g0 + PASSES // 2
+                for q in range(8):
+                    p0 = 32 * (q // 4) + q % 4
+                    nc.sync.dma_start(
+                        out=planes[p0:P:64, g0:g1, :],
+                        in_=rows[g0:g1, q:16:8, :].rearrange("g q n -> q g n"),
+                    )
+
+        def sort_words(u):
+            for b in range(BLOCKS):
+                x_words = sorted_pool.tile([P, UNIT_PASSES, 2, P], F32)
+                nc.vector.tensor_copy(
+                    out=x_words[:],
+                    in_=raw[(u, b)][:].bitcast(F32).rearrange("p (g q w) -> p g w q", g=UNIT_PASSES, w=2),
+                )
+                words[(u, b)] = x_words
+
+        def transpose_x(u):
+            for pair in range(UNIT_PAIRS):
+                x_grouped = mx_pool.tile([P, PAIR, ROWS, 4], BF16, align_bytes=64)
+                grouped[(u, pair)] = x_grouped
+                for i in range(PAIR):
+                    g = pair * PAIR + i
+                    for b0 in range(0, BLOCKS, 2):
+                        bank = banks.tile([P, 2, 2 * P], F32, tag="bank")
+                        for w in range(2):
+                            for b in (b0, b0 + 1):
+                                nc.tensor.transpose(
+                                    bank[:, w, (b - b0) * P : (b - b0 + 1) * P],
+                                    words[(u, b)][:, g, w, :],
+                                    ident_f32[:],
+                                )
+                        nc.scalar.copy(
+                            out=x_grouped[:].bitcast(F32)[:, i, b0 * P : (b0 + 2) * P, :],
+                            in_=bank[:].rearrange("p w r -> p r w"),
+                        )
+
+        def quantise_x(u):
+            for pair in range(UNIT_PAIRS):
+                x_codes = mx_pool.tile([P, PAIR * ROWS], U32, align_bytes=64)
+                x_scales = mx_pool.tile([P, PAIR * ROWS], U8, align_bytes=64)
+                nc.vector.quantize_mx(
+                    out=x_codes[:].bitcast(FP8X4),
+                    scales=x_scales[:],
+                    in_=grouped[(u, pair)][:].rearrange("p g r t -> p (g r t)"),
+                )
+                codes[(u, pair)] = (x_codes, x_scales)
+
+        def multiply(u):
+            half, c = divmod(u, UNITS_PER_HALF)
+            if c == 0:
+                sums_0 = sums_pool.tile([P, ROWS], F32)
+                sums_1 = sums_pool.tile([P, ROWS], F32)
+                sums[half] = (sums_0, sums_1)
+            for pair in range(UNIT_PAIRS):
+                x_codes, x_scales = codes[(u, pair)]
+                for i in range(PAIR):
+                    g = c * UNIT_PASSES + pair * PAIR + i
+                    for o in range(OUT_TILES):
+                        nc.tensor.matmul_mx(
+                            out=sums[half][o][:],
+                            lhsT=m_words[:, g, o * 2 * P : (o + 1) * 2 * P].bitcast(FP4X4),
+                            lhsT_scale=m_scales[:, g, o * P : (o + 1) * P],
+                            rhs=x_codes[:, i * ROWS : (i + 1) * ROWS].bitcast(FP8X4),
+                            rhs_scale=x_scales[:, i * ROWS : (i + 1) * ROWS],
+                            start=(g == 0),
+                            stop=(g == PASSES - 1),
+                        )
+
+        def copy_sums(half):
+            sb_0 = end_pool.tile([P, ROWS], F32)
+            sb_1 = end_pool.tile([P, ROWS], F32)
+            nc.scalar.copy(out=sb_0[:], in_=sums[half][0][:])
+            nc.vector.tensor_copy(out=sb_1[:], in_=sums[half][1][:])
+            sums_sb[half] = (sb_0, sb_1)
+
+        def finish_rows(half):
+            for b0 in range(0, BLOCKS, 2):
+                bank = banks.tile([P, 2, OUT_F], F32, tag="bank")
+                for b in (b0, b0 + 1):
+                    for o in range(OUT_TILES):
+                        nc.tensor.transpose(
+                            bank[:, b - b0, o * P : (o + 1) * P],
+                            sums_sb[half][o][:, b * P : (b + 1) * P],
+                            ident_f32[:],
+                        )
+                a0 = half * BLOCKS + b0
+                result = end_pool.tile([P, 2, OUT_F], F32)
+                nc.vector.scalar_tensor_tensor(
+                    out=result[:],
+                    in0=lora[:, a0 : a0 + 2, :],
+                    scalar=LORA_GAIN,
+                    in1=bank[:],
+                    op0=ALU.mult,
+                    op1=ALU.add,
+                )
+                nc.sync.dma_start(
+                    out=out[a0 * P : (a0 + 2) * P, :].rearrange("(b p) n -> p b n", p=P),
+                    in_=result[:],
+                )
+
+        load_x(0)
+        load_m_scales()
+        load_m_words(0)
+        h_rows = keep.tile([P, N_ADAPTERS, RANK], BF16)
+        nc.sync.dma_start(out=h_rows[:], in_=h_lora.rearrange("a b r -> b a r"))
+        b_rows = keep.tile([P, N_ADAPTERS, OUT_F], BF16)
+        nc.sync.dma_start(out=b_rows[:], in_=lora_B.rearrange("a r n -> r a n"))
+        for u in range(1, RAW_UNITS):
+            load_x(u)
+            load_m_words(u)
+        sort_words(0)
+        load_x(RAW_UNITS)
+        load_m_words(RAW_UNITS)
+
+        lora = keep.tile([P, N_ADAPTERS, OUT_F], F32)
+
+        def lora_products():
+            h_bank = banks.tile([P, N_ADAPTERS, P], BF16, tag="bank")
+            for a in range(N_ADAPTERS):
+                nc.tensor.transpose(h_bank[:, a, :], h_rows[:, a, :], ident_bf16[:])
+            h_cols = keep.tile([P, N_ADAPTERS, P], BF16)
+            nc.vector.tensor_copy(out=h_cols[:], in_=h_bank[:])
+            for a0 in range(0, N_ADAPTERS, 2):
+                bank = banks.tile([P, 2, OUT_F], F32, tag="bank")
+                for a in (a0, a0 + 1):
+                    nc.tensor.matmul(
+                        out=bank[:, a - a0, :], lhsT=h_cols[:, a, :], rhs=b_rows[:, a, :], start=True, stop=True
+                    )
+                nc.vector.tensor_copy(out=lora[:, a0 : a0 + 2, :], in_=bank[:])
+
+        for u in range(UNITS + 2):
+            if 1 <= u <= UNITS:
+                quantise_x(u - 1)
+            if u == 0:
+                transpose_x(0)
+                lora_products()
+            if u + 1 < UNITS:
+                sort_words(u + 1)
+            if u + 1 + RAW_UNITS < UNITS:
+                load_x(u + 1 + RAW_UNITS)
+                if u + 1 + RAW_UNITS < UNITS_PER_HALF:
+                    load_m_words(u + 1 + RAW_UNITS)
+            if 1 <= u < UNITS:
+                transpose_x(u)
+            if u >= 2 and (u - 1) % UNITS_PER_HALF == 0:
+                finish_rows((u - 2) // UNITS_PER_HALF)
+            if 1 <= u <= UNITS:
+                multiply(u - 1)
+                if u % UNITS_PER_HALF == 0:
+                    copy_sums(u // UNITS_PER_HALF - 1)

@@ -27,8 +27,13 @@ UNIT_PAIRS = 2
 UNIT_PASSES = PAIR * UNIT_PAIRS
 K_UNIT = UNIT_PASSES * K_PASS
 UNITS_PER_HALF = IN_F // K_UNIT
-UNITS = HALVES * UNITS_PER_HALF
 RAW_UNITS = 3
+UNIT_SIZES = [[UNIT_PASSES] * UNITS_PER_HALF, [UNIT_PASSES] * (UNITS_PER_HALF - 1) + [2, 1, 1]]
+UNIT_LIST = [
+    (half, sum(sizes[:i]), sizes[i]) for half, sizes in enumerate(UNIT_SIZES) for i in range(len(sizes))
+]
+UNITS = len(UNIT_LIST)
+LAST_OF_HALF = [len(UNIT_SIZES[0]) - 1, UNITS - 1]
 
 FLOPS = 2 * BATCH * IN_F * OUT_F + 2 * BATCH * RANK * OUT_F
 
@@ -62,11 +67,11 @@ def tile_lorasequential_pa_k_kernel(tc, x, h_lora, lora_B, M_words, M_scales, ou
         sums_sb = {}
 
         def load_x(u):
-            half, c = divmod(u, UNITS_PER_HALF)
+            half, g0, passes = UNIT_LIST[u]
             for b in range(BLOCKS):
                 r0 = half * ROWS + b * P
-                x_raw = raw_pool.tile([P, K_UNIT], BF16)
-                nc.sync.dma_start(out=x_raw[:], in_=x[r0 : r0 + P, c * K_UNIT : (c + 1) * K_UNIT])
+                x_raw = raw_pool.tile([P, passes * K_PASS], BF16)
+                nc.sync.dma_start(out=x_raw[:], in_=x[r0 : r0 + P, g0 * K_PASS : (g0 + passes) * K_PASS])
                 raw[(u, b)] = x_raw
 
         def load_m_words(c):
@@ -89,19 +94,24 @@ def tile_lorasequential_pa_k_kernel(tc, x, h_lora, lora_B, M_words, M_scales, ou
                     )
 
         def sort_words(u):
+            passes = UNIT_LIST[u][2]
             for b in range(BLOCKS):
-                x_words = sorted_pool.tile([P, UNIT_PASSES, 2, P], F32)
+                x_words = sorted_pool.tile([P, passes, 2, P], F32)
                 nc.vector.tensor_copy(
                     out=x_words[:],
-                    in_=raw[(u, b)][:].bitcast(F32).rearrange("p (g q w) -> p g w q", g=UNIT_PASSES, w=2),
+                    in_=raw[(u, b)][:].bitcast(F32).rearrange("p (g q w) -> p g w q", g=passes, w=2),
                 )
                 words[(u, b)] = x_words
 
+        def chunks(u):
+            passes = UNIT_LIST[u][2]
+            return [PAIR] * (passes // PAIR) + [1] * (passes % PAIR)
+
         def transpose_x(u):
-            for pair in range(UNIT_PAIRS):
-                x_grouped = mx_pool.tile([P, PAIR, ROWS, 4], BF16, align_bytes=64)
+            for pair, width in enumerate(chunks(u)):
+                x_grouped = mx_pool.tile([P, width, ROWS, 4], BF16, align_bytes=64)
                 grouped[(u, pair)] = x_grouped
-                for i in range(PAIR):
+                for i in range(width):
                     g = pair * PAIR + i
                     for b0 in range(0, BLOCKS, 2):
                         bank = banks.tile([P, 2, 2 * P], F32, tag="bank")
@@ -118,9 +128,9 @@ def tile_lorasequential_pa_k_kernel(tc, x, h_lora, lora_B, M_words, M_scales, ou
                         )
 
         def quantise_x(u):
-            for pair in range(UNIT_PAIRS):
-                x_codes = mx_pool.tile([P, PAIR * ROWS], U32, align_bytes=64)
-                x_scales = mx_pool.tile([P, PAIR * ROWS], U8, align_bytes=64)
+            for pair, width in enumerate(chunks(u)):
+                x_codes = mx_pool.tile([P, width * ROWS], U32, align_bytes=64)
+                x_scales = mx_pool.tile([P, width * ROWS], U8, align_bytes=64)
                 nc.vector.quantize_mx(
                     out=x_codes[:].bitcast(FP8X4),
                     scales=x_scales[:],
@@ -129,15 +139,15 @@ def tile_lorasequential_pa_k_kernel(tc, x, h_lora, lora_B, M_words, M_scales, ou
                 codes[(u, pair)] = (x_codes, x_scales)
 
         def multiply(u):
-            half, c = divmod(u, UNITS_PER_HALF)
-            if c == 0:
+            half, g0, passes = UNIT_LIST[u]
+            if g0 == 0:
                 sums_0 = sums_pool.tile([P, ROWS], F32)
                 sums_1 = sums_pool.tile([P, ROWS], F32)
                 sums[half] = (sums_0, sums_1)
-            for pair in range(UNIT_PAIRS):
+            for pair, width in enumerate(chunks(u)):
                 x_codes, x_scales = codes[(u, pair)]
-                for i in range(PAIR):
-                    g = c * UNIT_PASSES + pair * PAIR + i
+                for i in range(width):
+                    g = g0 + pair * PAIR + i
                     for o in range(OUT_TILES):
                         nc.tensor.matmul_mx(
                             out=sums[half][o][:],
@@ -225,9 +235,9 @@ def tile_lorasequential_pa_k_kernel(tc, x, h_lora, lora_B, M_words, M_scales, ou
                     load_m_words(u + 1 + RAW_UNITS)
             if 1 <= u < UNITS:
                 transpose_x(u)
-            if u >= 2 and (u - 1) % UNITS_PER_HALF == 0:
-                finish_rows((u - 2) // UNITS_PER_HALF)
+            if u - 2 in LAST_OF_HALF:
+                finish_rows(LAST_OF_HALF.index(u - 2))
             if 1 <= u <= UNITS:
                 multiply(u - 1)
-                if u % UNITS_PER_HALF == 0:
-                    copy_sums(u // UNITS_PER_HALF - 1)
+                if u - 1 in LAST_OF_HALF:
+                    copy_sums(LAST_OF_HALF.index(u - 1))

@@ -28,12 +28,13 @@ UNIT_PASSES = PAIR * UNIT_PAIRS
 K_UNIT = UNIT_PASSES * K_PASS
 UNITS_PER_HALF = IN_F // K_UNIT
 RAW_UNITS = 3
-UNIT_SIZES = [[UNIT_PASSES] * UNITS_PER_HALF, [UNIT_PASSES] * (UNITS_PER_HALF - 1) + [2, 1, 1]]
+UNIT_SIZES = [[2, 2] + [UNIT_PASSES] * (UNITS_PER_HALF - 1), [UNIT_PASSES] * UNITS_PER_HALF]
 UNIT_LIST = [
     (half, sum(sizes[:i]), sizes[i]) for half, sizes in enumerate(UNIT_SIZES) for i in range(len(sizes))
 ]
 UNITS = len(UNIT_LIST)
 LAST_OF_HALF = [len(UNIT_SIZES[0]) - 1, UNITS - 1]
+LORA_ROUND = 2
 
 FLOPS = 2 * BATCH * IN_F * OUT_F + 2 * BATCH * RANK * OUT_F
 
@@ -74,24 +75,20 @@ def tile_lorasequential_pa_k_kernel(tc, x, h_lora, lora_B, M_words, M_scales, ou
                 nc.sync.dma_start(out=x_raw[:], in_=x[r0 : r0 + P, g0 * K_PASS : (g0 + passes) * K_PASS])
                 raw[(u, b)] = x_raw
 
-        def load_m_words(c):
-            g0 = c * UNIT_PASSES
-            nc.sync.dma_start(
-                out=m_words[:, g0 : g0 + UNIT_PASSES, :].bitcast(I32),
-                in_=M_words.bitcast(I32)[g0 : g0 + UNIT_PASSES].rearrange("g p w -> p g w"),
-            )
-
-        def load_m_scales():
+        def load_m(u):
+            g0, passes = UNIT_LIST[u][1:]
+            g1 = g0 + passes
             planes = m_scales[:].bitcast(I32)
             rows = M_scales.bitcast(I32)
-            for g0 in range(0, PASSES, PASSES // 2):
-                g1 = g0 + PASSES // 2
-                for q in range(8):
-                    p0 = 32 * (q // 4) + q % 4
-                    nc.sync.dma_start(
-                        out=planes[p0:P:64, g0:g1, :],
-                        in_=rows[g0:g1, q:16:8, :].rearrange("g q n -> q g n"),
-                    )
+            for r in range(4):
+                nc.sync.dma_start(
+                    out=planes[r:P:32, g0:g1, :],
+                    in_=rows[g0:g1, r:16:4, :].rearrange("g q n -> q g n"),
+                )
+            nc.sync.dma_start(
+                out=m_words[:, g0:g1, :].bitcast(I32),
+                in_=M_words.bitcast(I32)[g0:g1].rearrange("g p w -> p g w"),
+            )
 
         def sort_words(u):
             passes = UNIT_LIST[u][2]
@@ -111,9 +108,9 @@ def tile_lorasequential_pa_k_kernel(tc, x, h_lora, lora_B, M_words, M_scales, ou
             for pair, width in enumerate(chunks(u)):
                 x_grouped = mx_pool.tile([P, width, ROWS, 4], BF16, align_bytes=64)
                 grouped[(u, pair)] = x_grouped
-                for i in range(width):
-                    g = pair * PAIR + i
-                    for b0 in range(0, BLOCKS, 2):
+                for b0 in range(0, BLOCKS, 2):
+                    for i in range(width):
+                        g = pair * PAIR + i
                         bank = banks.tile([P, 2, 2 * P], F32, tag="bank")
                         for w in range(2):
                             for b in (b0, b0 + 1):
@@ -191,19 +188,16 @@ def tile_lorasequential_pa_k_kernel(tc, x, h_lora, lora_B, M_words, M_scales, ou
                     in_=result[:],
                 )
 
-        load_x(0)
-        load_m_scales()
-        load_m_words(0)
         h_rows = keep.tile([P, N_ADAPTERS, RANK], BF16)
-        nc.sync.dma_start(out=h_rows[:], in_=h_lora.rearrange("a b r -> b a r"))
         b_rows = keep.tile([P, N_ADAPTERS, OUT_F], BF16)
-        nc.sync.dma_start(out=b_rows[:], in_=lora_B.rearrange("a r n -> r a n"))
-        for u in range(1, RAW_UNITS):
+        for u in range(RAW_UNITS):
             load_x(u)
-            load_m_words(u)
+            load_m(u)
+        nc.sync.dma_start(out=h_rows[:], in_=h_lora.rearrange("a b r -> b a r"))
+        nc.sync.dma_start(out=b_rows[:], in_=lora_B.rearrange("a r n -> r a n"))
         sort_words(0)
         load_x(RAW_UNITS)
-        load_m_words(RAW_UNITS)
+        load_m(RAW_UNITS)
 
         lora = keep.tile([P, N_ADAPTERS, OUT_F], F32)
 
@@ -221,19 +215,20 @@ def tile_lorasequential_pa_k_kernel(tc, x, h_lora, lora_B, M_words, M_scales, ou
                     )
                 nc.vector.tensor_copy(out=lora[:, a0 : a0 + 2, :], in_=bank[:])
 
-        for u in range(UNITS + 2):
-            if 1 <= u <= UNITS:
-                quantise_x(u - 1)
-            if u == 0:
-                transpose_x(0)
-                lora_products()
+        def prepare(u):
             if u + 1 < UNITS:
                 sort_words(u + 1)
             if u + 1 + RAW_UNITS < UNITS:
                 load_x(u + 1 + RAW_UNITS)
-                if u + 1 + RAW_UNITS < UNITS_PER_HALF:
-                    load_m_words(u + 1 + RAW_UNITS)
-            if 1 <= u < UNITS:
+                if UNIT_LIST[u + 1 + RAW_UNITS][0] == 0:
+                    load_m(u + 1 + RAW_UNITS)
+
+        for u in range(UNITS + 2):
+            if 1 <= u <= UNITS:
+                quantise_x(u - 1)
+            if u != LORA_ROUND:
+                prepare(u)
+            if u < UNITS:
                 transpose_x(u)
             if u - 2 in LAST_OF_HALF:
                 finish_rows(LAST_OF_HALF.index(u - 2))
@@ -241,3 +236,6 @@ def tile_lorasequential_pa_k_kernel(tc, x, h_lora, lora_B, M_words, M_scales, ou
                 multiply(u - 1)
                 if u - 1 in LAST_OF_HALF:
                     copy_sums(LAST_OF_HALF.index(u - 1))
+            if u == LORA_ROUND:
+                lora_products()
+                prepare(u)

@@ -102,7 +102,9 @@ def tile_lorasequential_pa_k_kernel(tc, x, h_lora, lora_B, M_words, M_scales, ou
 
         def chunks(u):
             passes = UNIT_LIST[u][2]
-            return [PAIR] * (passes // PAIR) + [1] * (passes % PAIR)
+            if u == UNITS - 1:
+                return [PAIR] * (passes // PAIR - 1) + [1, 1]
+            return [PAIR] * (passes // PAIR)
 
         def transpose_x(u):
             for pair, width in enumerate(chunks(u)):
@@ -110,7 +112,7 @@ def tile_lorasequential_pa_k_kernel(tc, x, h_lora, lora_B, M_words, M_scales, ou
                 grouped[(u, pair)] = x_grouped
                 for b0 in range(0, BLOCKS, 2):
                     for i in range(width):
-                        g = pair * PAIR + i
+                        g = sum(chunks(u)[:pair]) + i
                         bank = banks.tile([P, 2, 2 * P], F32, tag="bank")
                         for w in range(2):
                             for b in (b0, b0 + 1):
@@ -144,7 +146,7 @@ def tile_lorasequential_pa_k_kernel(tc, x, h_lora, lora_B, M_words, M_scales, ou
             for pair, width in enumerate(chunks(u)):
                 x_codes, x_scales = codes[(u, pair)]
                 for i in range(width):
-                    g = g0 + pair * PAIR + i
+                    g = g0 + sum(chunks(u)[:pair]) + i
                     for o in range(OUT_TILES):
                         nc.tensor.matmul_mx(
                             out=sums[half][o][:],
@@ -201,19 +203,22 @@ def tile_lorasequential_pa_k_kernel(tc, x, h_lora, lora_B, M_words, M_scales, ou
 
         lora = keep.tile([P, N_ADAPTERS, OUT_F], F32)
 
-        def lora_products():
+        h_cols = keep.tile([P, N_ADAPTERS, P], BF16)
+
+        def transpose_h():
             h_bank = banks.tile([P, N_ADAPTERS, P], BF16, tag="bank")
             for a in range(N_ADAPTERS):
                 nc.tensor.transpose(h_bank[:, a, :], h_rows[:, a, :], ident_bf16[:])
-            h_cols = keep.tile([P, N_ADAPTERS, P], BF16)
-            nc.vector.tensor_copy(out=h_cols[:], in_=h_bank[:])
+            nc.scalar.copy(out=h_cols[:], in_=h_bank[:])
+
+        def lora_products():
             for a0 in range(0, N_ADAPTERS, 2):
                 bank = banks.tile([P, 2, OUT_F], F32, tag="bank")
                 for a in (a0, a0 + 1):
                     nc.tensor.matmul(
                         out=bank[:, a - a0, :], lhsT=h_cols[:, a, :], rhs=b_rows[:, a, :], start=True, stop=True
                     )
-                nc.vector.tensor_copy(out=lora[:, a0 : a0 + 2, :], in_=bank[:])
+                nc.scalar.copy(out=lora[:, a0 : a0 + 2, :], in_=bank[:])
 
         def prepare(u):
             if u + 1 < UNITS:
@@ -226,10 +231,11 @@ def tile_lorasequential_pa_k_kernel(tc, x, h_lora, lora_B, M_words, M_scales, ou
         for u in range(UNITS + 2):
             if 1 <= u <= UNITS:
                 quantise_x(u - 1)
-            if u != LORA_ROUND:
-                prepare(u)
+            prepare(u)
             if u < UNITS:
                 transpose_x(u)
+            if u == LORA_ROUND:
+                transpose_h()
             if u - 2 in LAST_OF_HALF:
                 finish_rows(LAST_OF_HALF.index(u - 2))
             if 1 <= u <= UNITS:
@@ -238,4 +244,3 @@ def tile_lorasequential_pa_k_kernel(tc, x, h_lora, lora_B, M_words, M_scales, ou
                     copy_sums(LAST_OF_HALF.index(u - 1))
             if u == LORA_ROUND:
                 lora_products()
-                prepare(u)

@@ -34,6 +34,7 @@ UNIT_LIST = [
 ]
 UNITS = len(UNIT_LIST)
 LAST_OF_HALF = [len(UNIT_SIZES[0]) - 1, UNITS - 1]
+EARLY_UNITS = 6
 LORA_ROUND = 2
 
 FLOPS = 2 * BATCH * IN_F * OUT_F + 2 * BATCH * RANK * OUT_F
@@ -110,21 +111,25 @@ def tile_lorasequential_pa_k_kernel(tc, x, h_lora, lora_B, M_words, M_scales, ou
             for pair, width in enumerate(chunks(u)):
                 x_grouped = mx_pool.tile([P, width, ROWS, 4], BF16, align_bytes=64)
                 grouped[(u, pair)] = x_grouped
-                for b0 in range(0, BLOCKS, 2):
-                    for i in range(width):
-                        g = sum(chunks(u)[:pair]) + i
-                        bank = banks.tile([P, 2, 2 * P], F32, tag="bank")
-                        for w in range(2):
-                            for b in (b0, b0 + 1):
-                                nc.tensor.transpose(
-                                    bank[:, w, (b - b0) * P : (b - b0 + 1) * P],
-                                    words[(u, b)][:, g, w, :],
-                                    ident_f32[:],
-                                )
-                        nc.scalar.copy(
-                            out=x_grouped[:].bitcast(F32)[:, i, b0 * P : (b0 + 2) * P, :],
-                            in_=bank[:].rearrange("p w r -> p r w"),
+            pairs = list(enumerate(chunks(u)))
+            if u < EARLY_UNITS:
+                order = [(pair, i, b0) for b0 in range(0, BLOCKS, 2) for pair, width in pairs for i in range(width)]
+            else:
+                order = [(pair, i, b0) for pair, width in pairs for b0 in range(0, BLOCKS, 2) for i in range(width)]
+            for pair, i, b0 in order:
+                g = sum(chunks(u)[:pair]) + i
+                bank = banks.tile([P, 2, 2 * P], F32, tag="bank")
+                for w in range(2):
+                    for b in (b0, b0 + 1):
+                        nc.tensor.transpose(
+                            bank[:, w, (b - b0) * P : (b - b0 + 1) * P],
+                            words[(u, b)][:, g, w, :],
+                            ident_f32[:],
                         )
+                nc.scalar.copy(
+                    out=grouped[(u, pair)][:].bitcast(F32)[:, i, b0 * P : (b0 + 2) * P, :],
+                    in_=bank[:].rearrange("p w r -> p r w"),
+                )
 
         def quantise_x(u):
             for pair, width in enumerate(chunks(u)):
@@ -192,14 +197,15 @@ def tile_lorasequential_pa_k_kernel(tc, x, h_lora, lora_B, M_words, M_scales, ou
 
         h_rows = keep.tile([P, N_ADAPTERS, RANK], BF16)
         b_rows = keep.tile([P, N_ADAPTERS, OUT_F], BF16)
-        for u in range(RAW_UNITS):
+        load_x(0)
+        for u in range(1, RAW_UNITS):
             load_x(u)
-            load_m(u)
+            load_m(u - 1)
         nc.sync.dma_start(out=h_rows[:], in_=h_lora.rearrange("a b r -> b a r"))
         nc.sync.dma_start(out=b_rows[:], in_=lora_B.rearrange("a r n -> r a n"))
         sort_words(0)
         load_x(RAW_UNITS)
-        load_m(RAW_UNITS)
+        load_m(RAW_UNITS - 1)
 
         lora = keep.tile([P, N_ADAPTERS, OUT_F], F32)
 
@@ -225,8 +231,8 @@ def tile_lorasequential_pa_k_kernel(tc, x, h_lora, lora_B, M_words, M_scales, ou
                 sort_words(u + 1)
             if u + 1 + RAW_UNITS < UNITS:
                 load_x(u + 1 + RAW_UNITS)
-                if UNIT_LIST[u + 1 + RAW_UNITS][0] == 0:
-                    load_m(u + 1 + RAW_UNITS)
+                if UNIT_LIST[u + RAW_UNITS][0] == 0:
+                    load_m(u + RAW_UNITS)
 
         for u in range(UNITS + 2):
             if 1 <= u <= UNITS:

from contextlib import ExitStack

import concourse.mybir as mybir
from concourse.masks import make_identity

F32 = mybir.dt.float32
BF16 = mybir.dt.bfloat16
I32 = mybir.dt.int32
U32 = mybir.dt.uint32
U8 = mybir.dt.uint8
FP8X4 = mybir.dt.float8_e4m3fn_x4
FP4X4 = mybir.dt.float4_e2m1fn_x4
ALU = mybir.AluOpType

P = 128
BATCH, IN_F, OUT_F, RANK, N_ADAPTERS = 1024, 16384, 256, 128, 8
LORA_GAIN = 2.0

K_PASS = 4 * P
PASSES = IN_F // K_PASS
ROWS = 512
BLOCKS = ROWS // P
HALVES = BATCH // ROWS
OUT_TILES = OUT_F // P
PAIR = 2
UNIT_PAIRS = 2
UNIT_PASSES = PAIR * UNIT_PAIRS
K_UNIT = UNIT_PASSES * K_PASS
UNITS_PER_HALF = IN_F // K_UNIT
RAW_UNITS = 3
UNIT_SIZES = [[2, 2] + [UNIT_PASSES] * (UNITS_PER_HALF - 1), [UNIT_PASSES] * UNITS_PER_HALF]
UNIT_LIST = [
    (half, sum(sizes[:i]), sizes[i]) for half, sizes in enumerate(UNIT_SIZES) for i in range(len(sizes))
]
UNITS = len(UNIT_LIST)
LAST_OF_HALF = [len(UNIT_SIZES[0]) - 1, UNITS - 1]
EARLY_UNITS = 6
LORA_ROUND = 2

FLOPS = 2 * BATCH * IN_F * OUT_F + 2 * BATCH * RANK * OUT_F


def tile_lorasequential_pa_k_kernel(tc, x, h_lora, lora_B, M_words, M_scales, out):
    nc = tc.nc
    with ExitStack() as ctx:
        ctx.enter_context(tc.manual_schedule())
        keep = ctx.enter_context(tc.tile_pool(name="keep", bufs=1))
        raw_pool = ctx.enter_context(tc.tile_pool(name="raw", bufs=RAW_UNITS * BLOCKS))
        sorted_pool = ctx.enter_context(tc.tile_pool(name="sorted", bufs=2 * BLOCKS))
        mx_pool = ctx.enter_context(tc.tile_pool(name="mx", bufs=2 * UNIT_PAIRS))
        end_pool = ctx.enter_context(tc.tile_pool(name="end", bufs=2))
        banks = ctx.enter_context(tc.psum_pool(name="banks", bufs=6))
        sums_pool = ctx.enter_context(tc.psum_pool(name="sums", bufs=1))

        ident_f32 = keep.tile([P, P], F32)
        make_identity(nc, ident_f32[:])
        ident_bf16 = keep.tile([P, P], BF16)
        make_identity(nc, ident_bf16[:])

        m_words = keep.tile([P, PASSES, 2 * OUT_F], U8, align_bytes=64)
        m_scales = keep.tile([P, PASSES, OUT_F], U8, align_bytes=64)
        nc.vector.memset(m_scales[:].bitcast(I32), 0)

        raw = {}
        words = {}
        grouped = {}
        codes = {}
        sums = {}
        sums_sb = {}

        def load_x(u):
            half, g0, passes = UNIT_LIST[u]
            for b in range(BLOCKS):
                r0 = half * ROWS + b * P
                x_raw = raw_pool.tile([P, passes * K_PASS], BF16)
                nc.sync.dma_start(out=x_raw[:], in_=x[r0 : r0 + P, g0 * K_PASS : (g0 + passes) * K_PASS])
                raw[(u, b)] = x_raw

        def load_m(u):
            g0, passes = UNIT_LIST[u][1:]
            g1 = g0 + passes
            planes = m_scales[:].bitcast(I32)
            rows = M_scales.bitcast(I32)
            for r in range(4):
                nc.sync.dma_start(
                    out=planes[r:P:32, g0:g1, :],
                    in_=rows[g0:g1, r:16:4, :].rearrange("g q n -> q g n"),
                )
            nc.sync.dma_start(
                out=m_words[:, g0:g1, :].bitcast(I32),
                in_=M_words.bitcast(I32)[g0:g1].rearrange("g p w -> p g w"),
            )

        def sort_words(u):
            passes = UNIT_LIST[u][2]
            for b in range(BLOCKS):
                x_words = sorted_pool.tile([P, passes, 2, P], F32)
                nc.vector.tensor_copy(
                    out=x_words[:],
                    in_=raw[(u, b)][:].bitcast(F32).rearrange("p (g q w) -> p g w q", g=passes, w=2),
                )
                words[(u, b)] = x_words

        def chunks(u):
            passes = UNIT_LIST[u][2]
            if u == UNITS - 1:
                return [PAIR] * (passes // PAIR - 1) + [1, 1]
            return [PAIR] * (passes // PAIR)

        def transpose_x(u):
            for pair, width in enumerate(chunks(u)):
                x_grouped = mx_pool.tile([P, width, ROWS, 4], BF16, align_bytes=64)
                grouped[(u, pair)] = x_grouped
            pairs = list(enumerate(chunks(u)))
            if u < EARLY_UNITS:
                order = [(pair, i, b0) for b0 in range(0, BLOCKS, 2) for pair, width in pairs for i in range(width)]
            else:
                order = [(pair, i, b0) for pair, width in pairs for b0 in range(0, BLOCKS, 2) for i in range(width)]
            for pair, i, b0 in order:
                g = sum(chunks(u)[:pair]) + i
                bank = banks.tile([P, 2, 2 * P], F32, tag="bank")
                for w in range(2):
                    for b in (b0, b0 + 1):
                        nc.tensor.transpose(
                            bank[:, w, (b - b0) * P : (b - b0 + 1) * P],
                            words[(u, b)][:, g, w, :],
                            ident_f32[:],
                        )
                nc.scalar.copy(
                    out=grouped[(u, pair)][:].bitcast(F32)[:, i, b0 * P : (b0 + 2) * P, :],
                    in_=bank[:].rearrange("p w r -> p r w"),
                )

        def quantise_x(u):
            for pair, width in enumerate(chunks(u)):
                x_codes = mx_pool.tile([P, width * ROWS], U32, align_bytes=64)
                x_scales = mx_pool.tile([P, width * ROWS], U8, align_bytes=64)
                nc.vector.quantize_mx(
                    out=x_codes[:].bitcast(FP8X4),
                    scales=x_scales[:],
                    in_=grouped[(u, pair)][:].rearrange("p g r t -> p (g r t)"),
                )
                codes[(u, pair)] = (x_codes, x_scales)

        def multiply(u):
            half, g0, passes = UNIT_LIST[u]
            if g0 == 0:
                sums_0 = sums_pool.tile([P, ROWS], F32)
                sums_1 = sums_pool.tile([P, ROWS], F32)
                sums[half] = (sums_0, sums_1)
            for pair, width in enumerate(chunks(u)):
                x_codes, x_scales = codes[(u, pair)]
                for i in range(width):
                    g = g0 + sum(chunks(u)[:pair]) + i
                    for o in range(OUT_TILES):
                        nc.tensor.matmul_mx(
                            out=sums[half][o][:],
                            lhsT=m_words[:, g, o * 2 * P : (o + 1) * 2 * P].bitcast(FP4X4),
                            lhsT_scale=m_scales[:, g, o * P : (o + 1) * P],
                            rhs=x_codes[:, i * ROWS : (i + 1) * ROWS].bitcast(FP8X4),
                            rhs_scale=x_scales[:, i * ROWS : (i + 1) * ROWS],
                            start=(g == 0),
                            stop=(g == PASSES - 1),
                        )

        def copy_sums(half):
            sb_0 = end_pool.tile([P, ROWS], F32)
            sb_1 = end_pool.tile([P, ROWS], F32)
            nc.scalar.copy(out=sb_0[:], in_=sums[half][0][:])
            nc.vector.tensor_copy(out=sb_1[:], in_=sums[half][1][:])
            sums_sb[half] = (sb_0, sb_1)

        def finish_rows(half):
            for b0 in range(0, BLOCKS, 2):
                bank = banks.tile([P, 2, OUT_F], F32, tag="bank")
                for b in (b0, b0 + 1):
                    for o in range(OUT_TILES):
                        nc.tensor.transpose(
                            bank[:, b - b0, o * P : (o + 1) * P],
                            sums_sb[half][o][:, b * P : (b + 1) * P],
                            ident_f32[:],
                        )
                a0 = half * BLOCKS + b0
                result = end_pool.tile([P, 2, OUT_F], F32)
                nc.vector.scalar_tensor_tensor(
                    out=result[:],
                    in0=lora[:, a0 : a0 + 2, :],
                    scalar=LORA_GAIN,
                    in1=bank[:],
                    op0=ALU.mult,
                    op1=ALU.add,
                )
                nc.sync.dma_start(
                    out=out[a0 * P : (a0 + 2) * P, :].rearrange("(b p) n -> p b n", p=P),
                    in_=result[:],
                )

        h_rows = keep.tile([P, N_ADAPTERS, RANK], BF16)
        b_rows = keep.tile([P, N_ADAPTERS, OUT_F], BF16)
        load_x(0)
        for u in range(1, RAW_UNITS):
            load_x(u)
            load_m(u - 1)
        nc.sync.dma_start(out=h_rows[:], in_=h_lora.rearrange("a b r -> b a r"))
        nc.sync.dma_start(out=b_rows[:], in_=lora_B.rearrange("a r n -> r a n"))
        sort_words(0)
        load_x(RAW_UNITS)
        load_m(RAW_UNITS - 1)

        lora = keep.tile([P, N_ADAPTERS, OUT_F], F32)

        h_cols = keep.tile([P, N_ADAPTERS, P], BF16)

        def transpose_h():
            h_bank = banks.tile([P, N_ADAPTERS, P], BF16, tag="bank")
            for a in range(N_ADAPTERS):
                nc.tensor.transpose(h_bank[:, a, :], h_rows[:, a, :], ident_bf16[:])
            nc.scalar.copy(out=h_cols[:], in_=h_bank[:])

        def lora_products():
            for a0 in range(0, N_ADAPTERS, 2):
                bank = banks.tile([P, 2, OUT_F], F32, tag="bank")
                for a in (a0, a0 + 1):
                    nc.tensor.matmul(
                        out=bank[:, a - a0, :], lhsT=h_cols[:, a, :], rhs=b_rows[:, a, :], start=True, stop=True
                    )
                nc.scalar.copy(out=lora[:, a0 : a0 + 2, :], in_=bank[:])

        def prepare(u):
            if u + 1 < UNITS:
                sort_words(u + 1)
            if u + 1 + RAW_UNITS < UNITS:
                load_x(u + 1 + RAW_UNITS)
                if UNIT_LIST[u + RAW_UNITS][0] == 0:
                    load_m(u + RAW_UNITS)

        for u in range(UNITS + 2):
            if 1 <= u <= UNITS:
                quantise_x(u - 1)
            prepare(u)
            if u < UNITS:
                transpose_x(u)
            if u == LORA_ROUND:
                transpose_h()
            if u - 2 in LAST_OF_HALF:
                finish_rows(LAST_OF_HALF.index(u - 2))
            if 1 <= u <= UNITS:
                multiply(u - 1)
                if u - 1 in LAST_OF_HALF:
                    copy_sums(LAST_OF_HALF.index(u - 1))
            if u == LORA_ROUND:
                lora_products()
